import numpy as np
import ml_dtypes

BF16 = ml_dtypes.bfloat16


def bf(x):
    return np.asarray(x, np.float32).astype(BF16)


def f32(x):
    return np.asarray(x, np.float32)


def f64(x):
    return np.asarray(x).astype(np.float64)


def striped(idx):
    return np.tile(idx.reshape(-1, 16).T, (8, 1))


C, S, B, P, M, N = 128, 2048, 512, 3, 384, 1536


def setup_inputs():
    return {"emb": f32(np.random.standard_normal((C, S))), "pos_w": f32(0.5 * np.random.standard_normal((C, 1))), "pos_b": f32(0.5 * np.random.standard_normal((C, 1))), "w_in": bf(np.random.standard_normal((C, M)) / np.sqrt(C)), "b_in": f32(0.1 * np.random.standard_normal((M, 1))), "offs": striped(np.random.permutation(np.tile(np.arange(S), 2))[:N])}


def reference(emb, pos_w, pos_b, w_in, b_in, offs):
    idx = offs[:16].T.reshape(-1)
    place = np.repeat(np.arange(P, dtype=np.float64), B)[None, :]
    aug = f64(emb)[:, idx] + (place * f64(pos_w) + f64(pos_b))
    return f64(w_in).T @ aug + f64(b_in)

@@ -1,0 +1,70 @@
+import concourse.mybir as mybir
+
+F32 = mybir.dt.float32
+BF16 = mybir.dt.bfloat16
+U16 = mybir.dt.uint16
+ADD = mybir.AluOpType.add
+MULT = mybir.AluOpType.mult
+COPY = mybir.ActivationFunctionType.Copy
+IDENTITY = mybir.ActivationFunctionType.Identity
+
+C = 128
+S = 2048
+B = 512
+P = 3
+M = 384
+N = P * B
+BLOCKS = M // 128
+PER_COLUMN = 16
+
+FLOPS = 2 * C * M * N
+
+
+def tile_enhancedbrawlerpredictionmodel_kernel(tc, emb, pos_w, pos_b, w_in, b_in, offs, out):
+    nc = tc.nc
+    with (
+        tc.tile_pool(name="held", bufs=1) as held,
+        tc.tile_pool(name="work", bufs=3) as work,
+        tc.tile_pool(name="results", bufs=P * BLOCKS) as results,
+        tc.psum_pool(name="psum", bufs=8) as psum,
+    ):
+        offsets = held.tile([C, N // PER_COLUMN], U16, name="offsets")
+        nc.sync.dma_start(offsets[:], offs)
+        table = held.tile([C, S], F32, name="table")
+        nc.sync.dma_start(table[:], emb)
+        weights = held.tile([C, M], BF16, name="weights")
+        nc.scalar.dma_start(weights[:], w_in)
+        slope = held.tile([C, 1], F32, name="slope")
+        nc.scalar.dma_start(slope[:], pos_w)
+        base = held.tile([C, 1], F32, name="base")
+        nc.scalar.dma_start(base[:], pos_b)
+        biases = []
+        for k in range(BLOCKS):
+            bias = held.tile([128, 1], F32, name=f"bias{k}")
+            nc.scalar.dma_start(bias[:], b_in[k * 128 : (k + 1) * 128, :])
+            biases.append(bias)
+
+        place = held.tile([C, N], F32, name="place")
+        for p in range(P):
+            nc.gpsimd.memset(place[:, p * B : (p + 1) * B], float(p))
+        term = held.tile([C, N], F32, name="term")
+        nc.vector.tensor_scalar(term[:], place[:], slope[:], base[:], MULT, ADD)
+
+        for p in range(P):
+            piece = offsets[:, p * (B // PER_COLUMN) : (p + 1) * (B // PER_COLUMN)]
+            aug = work.tile([C, B], F32, name="aug")
+            nc.vector.tensor_tensor(aug[:], table[:].indirect(piece), term[:, p * B : (p + 1) * B], ADD)
+            rounded = work.tile([C, B], BF16, name="rounded")
+            nc.scalar.activation(rounded[:], aug[:], COPY)
+
+            for k in range(BLOCKS):
+                product = psum.tile([128, B], F32, name="product")
+                nc.tensor.matmul(
+                    product[:], weights[:, k * 128 : (k + 1) * 128], rounded[:], start=True, stop=True
+                )
+                result = results.tile([128, B], F32, name="result")
+                if k == BLOCKS - 1:
+                    nc.vector.tensor_scalar(result[:], product[:], biases[k][:], None, ADD)
+                else:
+                    nc.scalar.activation(result[:], product[:], IDENTITY, bias=biases[k][:])
+                nc.sync.dma_start(out[k * 128 : (k + 1) * 128, p * B : (p + 1) * B], result[:])

@@ -19,52 +19,65 @@ PER_COLUMN = 16
 
 FLOPS = 2 * C * M * N
 
+WIDTHS = (128, 128, 256, 512, 512)
+assert sum(WIDTHS) == N
+
 
 def tile_enhancedbrawlerpredictionmodel_kernel(tc, emb, pos_w, pos_b, w_in, b_in, offs, out):
     nc = tc.nc
     with (
         tc.tile_pool(name="held", bufs=1) as held,
+        tc.tile_pool(name="sums", bufs=1) as sums,
         tc.tile_pool(name="work", bufs=3) as work,
-        tc.tile_pool(name="results", bufs=P * BLOCKS) as results,
+        tc.tile_pool(name="results", bufs=len(WIDTHS) * BLOCKS) as results,
         tc.psum_pool(name="psum", bufs=8) as psum,
     ):
+        slope = held.tile([C, 1], F32, name="slope")
+        nc.sync.dma_start(slope[:], pos_w)
+        base = held.tile([C, 1], F32, name="base")
+        nc.sync.dma_start(base[:], pos_b)
         offsets = held.tile([C, N // PER_COLUMN], U16, name="offsets")
         nc.sync.dma_start(offsets[:], offs)
         table = held.tile([C, S], F32, name="table")
         nc.sync.dma_start(table[:], emb)
         weights = held.tile([C, M], BF16, name="weights")
         nc.scalar.dma_start(weights[:], w_in)
-        slope = held.tile([C, 1], F32, name="slope")
-        nc.scalar.dma_start(slope[:], pos_w)
-        base = held.tile([C, 1], F32, name="base")
-        nc.scalar.dma_start(base[:], pos_b)
         biases = []
         for k in range(BLOCKS):
             bias = held.tile([128, 1], F32, name=f"bias{k}")
             nc.scalar.dma_start(bias[:], b_in[k * 128 : (k + 1) * 128, :])
             biases.append(bias)
 
-        place = held.tile([C, N], F32, name="place")
-        for p in range(P):
-            nc.gpsimd.memset(place[:, p * B : (p + 1) * B], float(p))
-        term = held.tile([C, N], F32, name="term")
-        nc.vector.tensor_scalar(term[:], place[:], slope[:], base[:], MULT, ADD)
+        scratch = held.tile([C, 1], F32, name="scratch")
+        nc.gpsimd.memset(scratch[:], 0.0)
+        nc.scalar.activation(scratch[:], scratch[:], IDENTITY)
 
+        terms = []
         for p in range(P):
-            piece = offsets[:, p * (B // PER_COLUMN) : (p + 1) * (B // PER_COLUMN)]
-            aug = work.tile([C, B], F32, name="aug")
-            nc.vector.tensor_tensor(aug[:], table[:].indirect(piece), term[:, p * B : (p + 1) * B], ADD)
-            rounded = work.tile([C, B], BF16, name="rounded")
-            nc.scalar.activation(rounded[:], aug[:], COPY)
+            place = held.tile([C, B], F32, name=f"place{p}")
+            nc.gpsimd.memset(place[:], float(p))
+            term = held.tile([C, B], F32, name=f"term{p}")
+            nc.vector.tensor_scalar(term[:], place[:], slope[:], base[:], MULT, ADD)
+            terms.append(term)
+
+        start = 0
+        for width in WIDTHS:
+            entries = slice(start, start + width)
+            p, first = divmod(start, B)
+            piece = offsets[:, start // PER_COLUMN : (start + width) // PER_COLUMN]
+            aug = sums.tile([C, width], F32, name="aug")
+            nc.vector.tensor_tensor(aug[:], table[:].indirect(piece), terms[p][:, first : first + width], ADD)
+            rounded = work.tile([C, width], BF16, name="rounded")
+            nc.vector.tensor_copy(rounded[:], aug[:])
 
             for k in range(BLOCKS):
-                product = psum.tile([128, B], F32, name="product")
-                nc.tensor.matmul(
-                    product[:], weights[:, k * 128 : (k + 1) * 128], rounded[:], start=True, stop=True
-                )
-                result = results.tile([128, B], F32, name="result")
-                if k == BLOCKS - 1:
+                rows = slice(k * 128, (k + 1) * 128)
+                product = psum.tile([128, width], F32, name="product")
+                nc.tensor.matmul(product[:], weights[:, rows], rounded[:], start=True, stop=True)
+                result = results.tile([128, width], F32, name="result")
+                if start + width == N and k < BLOCKS - 1:
                     nc.vector.tensor_scalar(result[:], product[:], biases[k][:], None, ADD)
                 else:
                     nc.scalar.activation(result[:], product[:], IDENTITY, bias=biases[k][:])
-                nc.sync.dma_start(out[k * 128 : (k + 1) * 128, p * B : (p + 1) * B], result[:])
+                nc.sync.dma_start(out[rows, entries], result[:])
+            start += width

@@ -19,17 +19,16 @@ PER_COLUMN = 16
 
 FLOPS = 2 * C * M * N
 
-WIDTHS = (128, 128, 256, 512, 512)
-assert sum(WIDTHS) == N
+WIDTH = 256
+PIECES = N // WIDTH
 
 
 def tile_enhancedbrawlerpredictionmodel_kernel(tc, emb, pos_w, pos_b, w_in, b_in, offs, out):
     nc = tc.nc
     with (
         tc.tile_pool(name="held", bufs=1) as held,
-        tc.tile_pool(name="sums", bufs=1) as sums,
         tc.tile_pool(name="work", bufs=3) as work,
-        tc.tile_pool(name="results", bufs=len(WIDTHS) * BLOCKS) as results,
+        tc.tile_pool(name="results", bufs=PIECES * BLOCKS) as results,
         tc.psum_pool(name="psum", bufs=8) as psum,
     ):
         slope = held.tile([C, 1], F32, name="slope")
@@ -60,24 +59,28 @@ def tile_enhancedbrawlerpredictionmodel_kernel(tc, emb, pos_w, pos_b, w_in, b_in
             nc.vector.tensor_scalar(term[:], place[:], slope[:], base[:], MULT, ADD)
             terms.append(term)
 
-        start = 0
-        for width in WIDTHS:
-            entries = slice(start, start + width)
-            p, first = divmod(start, B)
-            piece = offsets[:, start // PER_COLUMN : (start + width) // PER_COLUMN]
-            aug = sums.tile([C, width], F32, name="aug")
-            nc.vector.tensor_tensor(aug[:], table[:].indirect(piece), terms[p][:, first : first + width], ADD)
-            rounded = work.tile([C, width], BF16, name="rounded")
+        def look_up(i):
+            p, first = divmod(i * WIDTH, B)
+            piece = offsets[:, i * WIDTH // PER_COLUMN : (i + 1) * WIDTH // PER_COLUMN]
+            aug = work.tile([C, WIDTH], F32, name="aug")
+            nc.vector.tensor_tensor(aug[:], table[:].indirect(piece), terms[p][:, first : first + WIDTH], ADD)
+            return aug
+
+        ahead = look_up(0)
+        for i in range(PIECES):
+            aug = ahead
+            if i + 1 < PIECES:
+                ahead = look_up(i + 1)
+            rounded = work.tile([C, WIDTH], BF16, name="rounded")
             nc.vector.tensor_copy(rounded[:], aug[:])
 
             for k in range(BLOCKS):
                 rows = slice(k * 128, (k + 1) * 128)
-                product = psum.tile([128, width], F32, name="product")
+                product = psum.tile([128, WIDTH], F32, name="product")
                 nc.tensor.matmul(product[:], weights[:, rows], rounded[:], start=True, stop=True)
-                result = results.tile([128, width], F32, name="result")
-                if start + width == N and k < BLOCKS - 1:
+                result = results.tile([128, WIDTH], F32, name="result")
+                if i >= PIECES - 2 and k < BLOCKS - 1:
                     nc.vector.tensor_scalar(result[:], product[:], biases[k][:], None, ADD)
                 else:
                     nc.scalar.activation(result[:], product[:], IDENTITY, bias=biases[k][:])
-                nc.sync.dma_start(out[rows, entries], result[:])
-            start += width
+                nc.sync.dma_start(out[rows, i * WIDTH : (i + 1) * WIDTH], result[:])

@@ -19,8 +19,9 @@ PER_COLUMN = 16
 
 FLOPS = 2 * C * M * N
 
-WIDTH = 256
-PIECES = N // WIDTH
+CUTS = (0, 256, 512, 768, 1024, 1280, 1536)
+PIECES = len(CUTS) - 1
+STORES = (256, 512, 1024, 1536)
 
 
 def tile_enhancedbrawlerpredictionmodel_kernel(tc, emb, pos_w, pos_b, w_in, b_in, offs, out):
@@ -28,7 +29,6 @@ def tile_enhancedbrawlerpredictionmodel_kernel(tc, emb, pos_w, pos_b, w_in, b_in
     with (
         tc.tile_pool(name="held", bufs=1) as held,
         tc.tile_pool(name="work", bufs=3) as work,
-        tc.tile_pool(name="results", bufs=PIECES * BLOCKS) as results,
         tc.psum_pool(name="psum", bufs=8) as psum,
     ):
         slope = held.tile([C, 1], F32, name="slope")
@@ -59,28 +59,40 @@ def tile_enhancedbrawlerpredictionmodel_kernel(tc, emb, pos_w, pos_b, w_in, b_in
             nc.vector.tensor_scalar(term[:], place[:], slope[:], base[:], MULT, ADD)
             terms.append(term)
 
+        results = [held.tile([128, N], F32, name=f"result{k}") for k in range(BLOCKS)]
+
         def look_up(i):
-            p, first = divmod(i * WIDTH, B)
-            piece = offsets[:, i * WIDTH // PER_COLUMN : (i + 1) * WIDTH // PER_COLUMN]
-            aug = work.tile([C, WIDTH], F32, name="aug")
-            nc.vector.tensor_tensor(aug[:], table[:].indirect(piece), terms[p][:, first : first + WIDTH], ADD)
+            start, end = CUTS[i], CUTS[i + 1]
+            p = start // B
+            aug = work.tile([C, end - start], F32, name="aug")
+            nc.vector.tensor_tensor(
+                aug[:],
+                table[:].indirect(offsets[:, start // PER_COLUMN : end // PER_COLUMN]),
+                terms[p][:, start - p * B : end - p * B],
+                ADD,
+            )
             return aug
 
         ahead = look_up(0)
+        stored = 0
         for i in range(PIECES):
+            start, end = CUTS[i], CUTS[i + 1]
             aug = ahead
             if i + 1 < PIECES:
                 ahead = look_up(i + 1)
-            rounded = work.tile([C, WIDTH], BF16, name="rounded")
+            rounded = work.tile([C, end - start], BF16, name="rounded")
             nc.vector.tensor_copy(rounded[:], aug[:])
 
             for k in range(BLOCKS):
-                rows = slice(k * 128, (k + 1) * 128)
-                product = psum.tile([128, WIDTH], F32, name="product")
-                nc.tensor.matmul(product[:], weights[:, rows], rounded[:], start=True, stop=True)
-                result = results.tile([128, WIDTH], F32, name="result")
+                product = psum.tile([128, end - start], F32, name="product")
+                nc.tensor.matmul(
+                    product[:], weights[:, k * 128 : (k + 1) * 128], rounded[:], start=True, stop=True
+                )
                 if i >= PIECES - 2 and k < BLOCKS - 1:
-                    nc.vector.tensor_scalar(result[:], product[:], biases[k][:], None, ADD)
+                    nc.vector.tensor_scalar(results[k][:, start:end], product[:], biases[k][:], None, ADD)
                 else:
-                    nc.scalar.activation(result[:], product[:], IDENTITY, bias=biases[k][:])
-                nc.sync.dma_start(out[rows, i * WIDTH : (i + 1) * WIDTH], result[:])
+                    nc.scalar.activation(results[k][:, start:end], product[:], IDENTITY, bias=biases[k][:])
+                if end in STORES:
+                    nc.sync.dma_start(out[k * 128 : (k + 1) * 128, stored:end], results[k][:, stored:end])
+            if end in STORES:
+                stored = end

@@ -19,9 +19,9 @@ PER_COLUMN = 16
 
 FLOPS = 2 * C * M * N
 
-CUTS = (0, 256, 512, 768, 1024, 1280, 1536)
-PIECES = len(CUTS) - 1
-STORES = (256, 512, 1024, 1536)
+WIDTH = 256
+PIECES = N // WIDTH
+WARM_UP = 10
 
 
 def tile_enhancedbrawlerpredictionmodel_kernel(tc, emb, pos_w, pos_b, w_in, b_in, offs, out):
@@ -29,7 +29,9 @@ def tile_enhancedbrawlerpredictionmodel_kernel(tc, emb, pos_w, pos_b, w_in, b_in
     with (
         tc.tile_pool(name="held", bufs=1) as held,
         tc.tile_pool(name="work", bufs=3) as work,
-        tc.psum_pool(name="psum", bufs=8) as psum,
+        tc.tile_pool(name="results", bufs=PIECES * BLOCKS) as results,
+        tc.psum_pool(name="psum", bufs=7) as psum,
+        tc.psum_pool(name="idle", bufs=1) as idle,
     ):
         slope = held.tile([C, 1], F32, name="slope")
         nc.sync.dma_start(slope[:], pos_w)
@@ -51,6 +53,12 @@ def tile_enhancedbrawlerpredictionmodel_kernel(tc, emb, pos_w, pos_b, w_in, b_in
         nc.gpsimd.memset(scratch[:], 0.0)
         nc.scalar.activation(scratch[:], scratch[:], IDENTITY)
 
+        zeros = held.tile([C, B], BF16, name="zeros")
+        nc.vector.memset(zeros[:], 0.0)
+        unread = idle.tile([128, B], F32, name="unread")
+        for repeat in range(WARM_UP):
+            nc.tensor.matmul(unread[:], zeros[:, 0:128], zeros[:], start=True, stop=True)
+
         terms = []
         for p in range(P):
             place = held.tile([C, B], F32, name=f"place{p}")
@@ -59,40 +67,28 @@ def tile_enhancedbrawlerpredictionmodel_kernel(tc, emb, pos_w, pos_b, w_in, b_in
             nc.vector.tensor_scalar(term[:], place[:], slope[:], base[:], MULT, ADD)
             terms.append(term)
 
-        results = [held.tile([128, N], F32, name=f"result{k}") for k in range(BLOCKS)]
-
         def look_up(i):
-            start, end = CUTS[i], CUTS[i + 1]
-            p = start // B
-            aug = work.tile([C, end - start], F32, name="aug")
-            nc.vector.tensor_tensor(
-                aug[:],
-                table[:].indirect(offsets[:, start // PER_COLUMN : end // PER_COLUMN]),
-                terms[p][:, start - p * B : end - p * B],
-                ADD,
-            )
+            p, first = divmod(i * WIDTH, B)
+            piece = offsets[:, i * WIDTH // PER_COLUMN : (i + 1) * WIDTH // PER_COLUMN]
+            aug = work.tile([C, WIDTH], F32, name="aug")
+            nc.vector.tensor_tensor(aug[:], table[:].indirect(piece), terms[p][:, first : first + WIDTH], ADD)
             return aug
 
         ahead = look_up(0)
-        stored = 0
         for i in range(PIECES):
-            start, end = CUTS[i], CUTS[i + 1]
             aug = ahead
             if i + 1 < PIECES:
                 ahead = look_up(i + 1)
-            rounded = work.tile([C, end - start], BF16, name="rounded")
+            rounded = work.tile([C, WIDTH], BF16, name="rounded")
             nc.vector.tensor_copy(rounded[:], aug[:])
 
             for k in range(BLOCKS):
-                product = psum.tile([128, end - start], F32, name="product")
-                nc.tensor.matmul(
-                    product[:], weights[:, k * 128 : (k + 1) * 128], rounded[:], start=True, stop=True
-                )
+                rows = slice(k * 128, (k + 1) * 128)
+                product = psum.tile([128, WIDTH], F32, name="product")
+                nc.tensor.matmul(product[:], weights[:, rows], rounded[:], start=True, stop=True)
+                result = results.tile([128, WIDTH], F32, name="result")
                 if i >= PIECES - 2 and k < BLOCKS - 1:
-                    nc.vector.tensor_scalar(results[k][:, start:end], product[:], biases[k][:], None, ADD)
+                    nc.vector.tensor_scalar(result[:], product[:], biases[k][:], None, ADD)
                 else:
-                    nc.scalar.activation(results[k][:, start:end], product[:], IDENTITY, bias=biases[k][:])
-                if end in STORES:
-                    nc.sync.dma_start(out[k * 128 : (k + 1) * 128, stored:end], results[k][:, stored:end])
-            if end in STORES:
-                stored = end
+                    nc.scalar.activation(result[:], product[:], IDENTITY, bias=biases[k][:])
+                nc.sync.dma_start(out[rows, i * WIDTH : (i + 1) * WIDTH], result[:])

@@ -19,9 +19,9 @@ PER_COLUMN = 16
 
 FLOPS = 2 * C * M * N
 
-WIDTH = 256
-PIECES = N // WIDTH
-WARM_UP = 10
+CUTS = (0, 128, 256, 512, 768, 1024, 1280, 1536)
+PIECES = len(CUTS) - 1
+SHORT = 2
 
 
 def tile_enhancedbrawlerpredictionmodel_kernel(tc, emb, pos_w, pos_b, w_in, b_in, offs, out):
@@ -30,8 +30,7 @@ def tile_enhancedbrawlerpredictionmodel_kernel(tc, emb, pos_w, pos_b, w_in, b_in
         tc.tile_pool(name="held", bufs=1) as held,
         tc.tile_pool(name="work", bufs=3) as work,
         tc.tile_pool(name="results", bufs=PIECES * BLOCKS) as results,
-        tc.psum_pool(name="psum", bufs=7) as psum,
-        tc.psum_pool(name="idle", bufs=1) as idle,
+        tc.psum_pool(name="psum", bufs=8) as psum,
     ):
         slope = held.tile([C, 1], F32, name="slope")
         nc.sync.dma_start(slope[:], pos_w)
@@ -53,12 +52,6 @@ def tile_enhancedbrawlerpredictionmodel_kernel(tc, emb, pos_w, pos_b, w_in, b_in
         nc.gpsimd.memset(scratch[:], 0.0)
         nc.scalar.activation(scratch[:], scratch[:], IDENTITY)
 
-        zeros = held.tile([C, B], BF16, name="zeros")
-        nc.vector.memset(zeros[:], 0.0)
-        unread = idle.tile([128, B], F32, name="unread")
-        for repeat in range(WARM_UP):
-            nc.tensor.matmul(unread[:], zeros[:, 0:128], zeros[:], start=True, stop=True)
-
         terms = []
         for p in range(P):
             place = held.tile([C, B], F32, name=f"place{p}")
@@ -68,27 +61,36 @@ def tile_enhancedbrawlerpredictionmodel_kernel(tc, emb, pos_w, pos_b, w_in, b_in
             terms.append(term)
 
         def look_up(i):
-            p, first = divmod(i * WIDTH, B)
-            piece = offsets[:, i * WIDTH // PER_COLUMN : (i + 1) * WIDTH // PER_COLUMN]
-            aug = work.tile([C, WIDTH], F32, name="aug")
-            nc.vector.tensor_tensor(aug[:], table[:].indirect(piece), terms[p][:, first : first + WIDTH], ADD)
+            start, end = CUTS[i], CUTS[i + 1]
+            p = start // B
+            aug = work.tile([C, end - start], F32, name="aug")
+            nc.vector.tensor_tensor(
+                aug[:],
+                table[:].indirect(offsets[:, start // PER_COLUMN : end // PER_COLUMN]),
+                terms[p][:, start - p * B : end - p * B],
+                ADD,
+            )
             return aug
 
         ahead = look_up(0)
         for i in range(PIECES):
+            start, end = CUTS[i], CUTS[i + 1]
             aug = ahead
             if i + 1 < PIECES:
                 ahead = look_up(i + 1)
-            rounded = work.tile([C, WIDTH], BF16, name="rounded")
-            nc.vector.tensor_copy(rounded[:], aug[:])
+            rounded = work.tile([C, end - start], BF16, name="rounded")
+            if i < SHORT:
+                nc.scalar.activation(rounded[:], aug[:], IDENTITY)
+            else:
+                nc.vector.tensor_copy(rounded[:], aug[:])
 
             for k in range(BLOCKS):
                 rows = slice(k * 128, (k + 1) * 128)
-                product = psum.tile([128, WIDTH], F32, name="product")
+                product = psum.tile([128, end - start], F32, name="product")
                 nc.tensor.matmul(product[:], weights[:, rows], rounded[:], start=True, stop=True)
-                result = results.tile([128, WIDTH], F32, name="result")
+                result = results.tile([128, end - start], F32, name="result")
                 if i >= PIECES - 2 and k < BLOCKS - 1:
                     nc.vector.tensor_scalar(result[:], product[:], biases[k][:], None, ADD)
                 else:
                     nc.scalar.activation(result[:], product[:], IDENTITY, bias=biases[k][:])
-                nc.sync.dma_start(out[rows, i * WIDTH : (i + 1) * WIDTH], result[:])
+                nc.sync.dma_start(out[rows, start:end], result[:])

@@ -32,14 +32,14 @@ def tile_enhancedbrawlerpredictionmodel_kernel(tc, emb, pos_w, pos_b, w_in, b_in
         tc.tile_pool(name="results", bufs=PIECES * BLOCKS) as results,
         tc.psum_pool(name="psum", bufs=8) as psum,
     ):
-        slope = held.tile([C, 1], F32, name="slope")
-        nc.sync.dma_start(slope[:], pos_w)
-        base = held.tile([C, 1], F32, name="base")
-        nc.sync.dma_start(base[:], pos_b)
         offsets = held.tile([C, N // PER_COLUMN], U16, name="offsets")
         nc.sync.dma_start(offsets[:], offs)
         table = held.tile([C, S], F32, name="table")
         nc.sync.dma_start(table[:], emb)
+        slope = held.tile([C, 1], F32, name="slope")
+        nc.scalar.dma_start(slope[:], pos_w)
+        base = held.tile([C, 1], F32, name="base")
+        nc.scalar.dma_start(base[:], pos_b)
         weights = held.tile([C, M], BF16, name="weights")
         nc.scalar.dma_start(weights[:], w_in)
         biases = []

@@ -89,7 +89,7 @@ def tile_enhancedbrawlerpredictionmodel_kernel(tc, emb, pos_w, pos_b, w_in, b_in
                 product = psum.tile([128, end - start], F32, name="product")
                 nc.tensor.matmul(product[:], weights[:, rows], rounded[:], start=True, stop=True)
                 result = results.tile([128, end - start], F32, name="result")
-                if i >= PIECES - 2 and k < BLOCKS - 1:
+                if i == PIECES - 1 and k < BLOCKS - 1:
                     nc.vector.tensor_scalar(result[:], product[:], biases[k][:], None, ADD)
                 else:
                     nc.scalar.activation(result[:], product[:], IDENTITY, bias=biases[k][:])

@@ -36,12 +36,12 @@ def tile_enhancedbrawlerpredictionmodel_kernel(tc, emb, pos_w, pos_b, w_in, b_in
         nc.sync.dma_start(offsets[:], offs)
         table = held.tile([C, S], F32, name="table")
         nc.sync.dma_start(table[:], emb)
+        weights = held.tile([C, M], BF16, name="weights")
+        nc.sync.dma_start(weights[:], w_in)
         slope = held.tile([C, 1], F32, name="slope")
         nc.scalar.dma_start(slope[:], pos_w)
         base = held.tile([C, 1], F32, name="base")
         nc.scalar.dma_start(base[:], pos_b)
-        weights = held.tile([C, M], BF16, name="weights")
-        nc.scalar.dma_start(weights[:], w_in)
         biases = []
         for k in range(BLOCKS):
             bias = held.tile([128, 1], F32, name=f"bias{k}")

@@ -45,7 +45,7 @@ def tile_enhancedbrawlerpredictionmodel_kernel(tc, emb, pos_w, pos_b, w_in, b_in
         biases = []
         for k in range(BLOCKS):
             bias = held.tile([128, 1], F32, name=f"bias{k}")
-            nc.scalar.dma_start(bias[:], b_in[k * 128 : (k + 1) * 128, :])
+            nc.sync.dma_start(bias[:], b_in[k * 128 : (k + 1) * 128, :])
             biases.append(bias)
 
         scratch = held.tile([C, 1], F32, name="scratch")

import concourse.mybir as mybir

F32 = mybir.dt.float32
BF16 = mybir.dt.bfloat16
U16 = mybir.dt.uint16
ADD = mybir.AluOpType.add
MULT = mybir.AluOpType.mult
COPY = mybir.ActivationFunctionType.Copy
IDENTITY = mybir.ActivationFunctionType.Identity

C = 128
S = 2048
B = 512
P = 3
M = 384
N = P * B
BLOCKS = M // 128
PER_COLUMN = 16

FLOPS = 2 * C * M * N

CUTS = (0, 128, 256, 512, 768, 1024, 1280, 1536)
PIECES = len(CUTS) - 1
SHORT = 2


def tile_enhancedbrawlerpredictionmodel_kernel(tc, emb, pos_w, pos_b, w_in, b_in, offs, out):
    nc = tc.nc
    with (
        tc.tile_pool(name="held", bufs=1) as held,
        tc.tile_pool(name="work", bufs=3) as work,
        tc.tile_pool(name="results", bufs=PIECES * BLOCKS) as results,
        tc.psum_pool(name="psum", bufs=8) as psum,
    ):
        offsets = held.tile([C, N // PER_COLUMN], U16, name="offsets")
        nc.sync.dma_start(offsets[:], offs)
        table = held.tile([C, S], F32, name="table")
        nc.sync.dma_start(table[:], emb)
        weights = held.tile([C, M], BF16, name="weights")
        nc.sync.dma_start(weights[:], w_in)
        slope = held.tile([C, 1], F32, name="slope")
        nc.scalar.dma_start(slope[:], pos_w)
        base = held.tile([C, 1], F32, name="base")
        nc.scalar.dma_start(base[:], pos_b)
        biases = []
        for k in range(BLOCKS):
            bias = held.tile([128, 1], F32, name=f"bias{k}")
            nc.sync.dma_start(bias[:], b_in[k * 128 : (k + 1) * 128, :])
            biases.append(bias)

        scratch = held.tile([C, 1], F32, name="scratch")
        nc.gpsimd.memset(scratch[:], 0.0)
        nc.scalar.activation(scratch[:], scratch[:], IDENTITY)

        terms = []
        for p in range(P):
            place = held.tile([C, B], F32, name=f"place{p}")
            nc.gpsimd.memset(place[:], float(p))
            term = held.tile([C, B], F32, name=f"term{p}")
            nc.vector.tensor_scalar(term[:], place[:], slope[:], base[:], MULT, ADD)
            terms.append(term)

        def look_up(i):
            start, end = CUTS[i], CUTS[i + 1]
            p = start // B
            aug = work.tile([C, end - start], F32, name="aug")
            nc.vector.tensor_tensor(
                aug[:],
                table[:].indirect(offsets[:, start // PER_COLUMN : end // PER_COLUMN]),
                terms[p][:, start - p * B : end - p * B],
                ADD,
            )
            return aug

        ahead = look_up(0)
        for i in range(PIECES):
            start, end = CUTS[i], CUTS[i + 1]
            aug = ahead
            if i + 1 < PIECES:
                ahead = look_up(i + 1)
            rounded = work.tile([C, end - start], BF16, name="rounded")
            if i < SHORT:
                nc.scalar.activation(rounded[:], aug[:], IDENTITY)
            else:
                nc.vector.tensor_copy(rounded[:], aug[:])

            for k in range(BLOCKS):
                rows = slice(k * 128, (k + 1) * 128)
                product = psum.tile([128, end - start], F32, name="product")
                nc.tensor.matmul(product[:], weights[:, rows], rounded[:], start=True, stop=True)
                result = results.tile([128, end - start], F32, name="result")
                if i == PIECES - 1 and k < BLOCKS - 1:
                    nc.vector.tensor_scalar(result[:], product[:], biases[k][:], None, ADD)
                else:
                    nc.scalar.activation(result[:], product[:], IDENTITY, bias=biases[k][:])
                nc.sync.dma_start(out[rows, start:end], result[:])
